import numpy as np
import ml_dtypes


def mxq(x, axis, fmt="e4m3"):
    dtype, down = {"e4m3": (ml_dtypes.float8_e4m3fn, 7), "e5m2": (ml_dtypes.float8_e5m2, 14)}[fmt]
    v = np.moveaxis(np.asarray(x, np.float32).astype(ml_dtypes.bfloat16).astype(np.float64), axis, -1)
    blocks = v.reshape(v.shape[:-1] + (-1, 32))
    amax = np.abs(blocks).max(-1, keepdims=True)
    byte = np.maximum(np.where(amax > 0, np.frexp(amax)[1] - 1 + 127, 0) - down, 1)
    scale = np.exp2(byte - 127.0)
    codes = (blocks / scale).astype(np.float32).astype(dtype).astype(np.float64)
    return np.moveaxis((codes * scale).reshape(v.shape), -1, axis)


WIDE = False


def mx_kscale(k):
    if not WIDE:
        return np.ones(k)
    levels = np.array([10, -10, 5, -5, 0])
    a = np.random.permutation(np.resize(levels, k // 512 * 4)).reshape(k // 512, 4)
    idx = np.arange(k)
    return np.exp2(a[idx // 512, idx % 128 // 32])


BF16 = ml_dtypes.bfloat16


def bf(x):
    return np.asarray(x, np.float32).astype(BF16)


def f64(x):
    return np.asarray(x).astype(np.float64)


B, C, T, P, N, D = 8, 16, 2048, 128, 8, 512
L = T // P
G = L // N


def setup_inputs():
    s = mx_kscale(D)
    u = mx_kscale(P * N)
    un = u.reshape(P, N).T
    ut = np.tile(u, G)
    return {'h_enc': bf(np.random.standard_normal((N, B, C, G, D)) * 0.7 * s),
            'dec_W': bf(np.random.standard_normal((N, D, P)) / np.sqrt(D) / s[None, :, None] * un[:, None, :]),
            'dec_b': bf(np.random.standard_normal((N, P)) * 0.2 * un),
            'map_W': bf(np.random.standard_normal((T, T)) / np.sqrt(T) / ut[:, None]),
            'map_b': bf(np.random.standard_normal(T) * 0.2)}


def reference(h_enc, dec_W, dec_b, map_W, map_b):
    h = f64(h_enc).reshape(N, B * C * G, D)
    r = (mxq(h, 2, 'e4m3') @ mxq(f64(dec_W), 1, 'e4m3')) + f64(dec_b)[:, None, :]
    r = r.reshape(N, B, C, G * P)
    x_rec = np.moveaxis(r, 0, -1).reshape(B * C, T)
    y_hat = (mxq(x_rec, 1, 'e4m3') @ mxq(f64(map_W), 0, 'e4m3')) + f64(map_b)
    return y_hat.reshape(B, C, T)

@@ -1,0 +1,196 @@
+from contextlib import ExitStack
+
+import concourse.mybir as mybir
+from concourse.masks import make_identity
+
+F32 = mybir.dt.float32
+BF16 = mybir.dt.bfloat16
+U32 = mybir.dt.uint32
+U8 = mybir.dt.uint8
+I32 = mybir.dt.int32
+FP8X4 = mybir.dt.float8_e4m3fn_x4
+ADD = mybir.AluOpType.add
+
+P = 128
+FLOPS = 2 * 2048 * 512 * 128 + 2 * 128 * 2048 * 2048
+
+MANUAL = True
+LOADS = [("h", 0), ("d", 0), ("d", 1), ("h", 1), ("h", 2), ("h", 3), ("w", 0, 0, 1024), ("w", 0, 1024, 1024), ("w", 1, 0, 2048), ("w", 2, 0, 2048), ("w", 3, 0, 1024), ("w", 3, 1024, 512), ("w", 3, 1536, 512)]
+ORDER = [("TH", 0, 0), ("BX1",), ("TH", 0, 1), ("EH", 0, 0, "S"), ("BXT",), ("EH", 0, 1, "S"), ("RD", 0, "V"), ("BYm", 0), ("BYm", 1), ("EBY", 0, "S"), ("RD", 1, "S"), ("BX2",), ("QH", 0), ("QD", 0), ("TH", 1, 0), ("TH", 1, 1), ("TH", 2, 0), ("TH", 2, 1), ("EH", 1, 0, "S"), ("QD", 1), ("TH", 3, 0), ("EH", 1, 1, "S"), ("TH", 3, 1), ("EH", 2, 0, "S"), ("QH", 1), ("S1", 0), ("EH", 3, 0, "S"), ("EH", 2, 1, "V"), ("EH", 3, 1, "S"), ("QH", 2), ("EBY", 1, "S"), ("S1", 1), ("QH", 3), ("RW", 0, 1, "S"), ("RW", 0, 0, "V"), ("S1", 2), ("QW", 0, 0), ("RW", 0, 2, "V"), ("S1", 3), ("RW", 0, 3, "S"), ("QW", 0, 1), ("EX", 0), ("EX", 1), ("EX", 2), ("EX", 3), ("RW", 1, 0, "S"), ("QW", 0, 2), ("QX",), ("QW", 0, 3), ("MM", 0, 0), ("RW", 1, 2, "V"), ("MM", 0, 1), ("MM", 0, 2), ("RW", 1, 1, "S"), ("MM", 0, 3), ("QW", 1, 0), ("QW", 1, 2), ("MM", 1, 0), ("RW", 1, 3, "S"), ("RW", 2, 2, "V"), ("MM", 1, 2), ("QW", 1, 1), ("QW", 2, 2), ("MM", 1, 1), ("RW", 2, 0, "S"), ("QW", 1, 3), ("MM", 2, 2), ("RW", 3, 0, "V"), ("MM", 1, 3), ("RW", 3, 1, "V"), ("RW", 2, 1, "S"), ("QW", 2, 0), ("QW", 3, 0), ("MM", 2, 0), ("QW", 3, 1), ("RW", 2, 3, "S"), ("MM", 3, 0), ("QW", 2, 1), ("MM", 3, 1), ("RW", 3, 2, "V"), ("MM", 2, 1), ("EY", 0), ("RW", 3, 3, "S"), ("QW", 2, 3), ("QW", 3, 2), ("MM", 2, 3), ("EY", 1), ("MM", 3, 2), ("QW", 3, 3), ("EY", 2), ("MM", 3, 3), ("EY", 3)]
+
+
+def tile_model_pb_kernel(tc, h_enc, dec_W, dec_b, map_W, map_b, out):
+    nc = tc.nc
+    with ExitStack() as ctx:
+        const = ctx.enter_context(tc.tile_pool(name="const", bufs=1))
+        stage = ctx.enter_context(tc.tile_pool(name="stage", bufs=6))
+        psum = ctx.enter_context(tc.psum_pool(name="psum", bufs=8))
+        if MANUAL:
+            ctx.enter_context(tc.manual_schedule())
+
+        ident = const.tile([P, P], F32, name="ident")
+        make_identity(nc, ident[:])
+        t1 = const.tile([P, 128], BF16, name="t1")
+        nc.gpsimd.memset(t1[:].bitcast(F32), 0.0)
+        zb = const.tile([P, 2048], BF16, name="zb")
+        nc.gpsimd.memset(zb[:].bitcast(F32), 0.0)
+        dbv = dec_b.rearrange("(h j) (c p) -> c j h p", h=2, c=2)
+        for cp in range(2):
+            nc.gpsimd.dma_start(
+                out=t1[4 * cp:4 * cp + 4, :].rearrange("r (h p) -> r h p", h=2), in_=dbv[cp])
+        nc.gpsimd.dma_start(out=zb[0:1, :], in_=map_b.rearrange("(o s) -> o s", o=1))
+        ones = const.tile([P, P], BF16, name="ones")
+        nc.vector.memset(ones[:], 1.0)
+        dgr = [const.tile([P, 4096], BF16, name="dgr%d" % hh, align_bytes=64) for hh in range(2)]
+        for hh in range(2):
+            nc.vector.memset(dgr[hh][:].bitcast(I32), 0)
+
+        hv = h_enc.rearrange("(h j) b c l d -> j (b c) h (l d)", h=2)
+        dv = dec_W.rearrange("(h j) (q t) p -> h q j (t p)", h=2, t=4)
+        wv = map_W.rearrange("(c m j) s -> c m j s", m=P, j=4)
+        hraw = [const.tile([P, 2048], BF16, name="hraw%d" % j) for j in range(4)]
+        draw = [const.tile([P, 2048], BF16, name="draw%d" % hh) for hh in range(2)]
+        wsrc = {}
+        for ld in LOADS:
+            if ld[0] == "h":
+                nc.sync.dma_start(out=hraw[ld[1]][:].rearrange("p (h x) -> p h x", h=2), in_=hv[ld[1]])
+            elif ld[0] == "d":
+                nc.sync.dma_start(out=draw[ld[1]][:].rearrange("p (j x) -> p j x", j=4), in_=dv[ld[1]])
+            else:
+                c, s0, width = ld[1], ld[2], ld[3]
+                wraw = const.tile([P, 4, width], BF16, name="wraw%d_%d" % (c, s0))
+                nc.sync.dma_start(out=wraw[:], in_=wv[c][:, :, s0:s0 + width])
+                for k in range(s0 // 512, (s0 + width) // 512):
+                    wsrc[(c, k)] = wraw[:, :, 512 * k - s0:512 * k - s0 + 512]
+
+        by = const.tile([P, 2048], BF16, name="by")
+        t2 = const.tile([P, 128], F32, name="t2")
+        bx = const.tile([P, 8], F32, name="bx")
+        dw = [const.tile([P, 1024], U32, name="dw%d" % hh, align_bytes=64) for hh in range(2)]
+        dsc = [const.tile([P, 1024], U8, name="dsc%d" % hh, align_bytes=64) for hh in range(2)]
+        hw = [const.tile([P, 512], U32, name="hw%d" % j, align_bytes=64) for j in range(4)]
+        hsc = [const.tile([P, 512], U8, name="hsc%d" % j, align_bytes=64) for j in range(4)]
+        hgr = [const.tile([P, 2048], BF16, name="hgr%d" % j, align_bytes=64) for j in range(4)]
+        xgr = const.tile([P, 2048], BF16, name="xgr", align_bytes=64)
+        xw = const.tile([P, 512], U32, name="xw", align_bytes=64)
+        xsc = const.tile([P, 512], U8, name="xsc", align_bytes=64)
+        ov = out.rearrange("b c s -> (b c) s")
+        live = {}
+
+        def copy_on(eng, dst, src):
+            if eng == "V":
+                nc.vector.tensor_copy(out=dst, in_=src)
+            else:
+                nc.scalar.copy(out=dst, in_=src)
+
+        def op_BYm(g):
+            pby = psum.tile([P, 1024], BF16, name="pby", tag="ps")
+            live[("pby", g)] = pby
+            for e in range(2):
+                nc.tensor.matmul(out=pby[:, 512 * e:512 * e + 512], lhsT=ones[:],
+                                 rhs=zb[:, 1024 * g + 512 * e:1024 * g + 512 * e + 512],
+                                 start=True, stop=True)
+
+        def op_EBY(g, eng):
+            copy_on(eng, by[:, 1024 * g:1024 * g + 1024], live[("pby", g)][:])
+
+        def op_BX1():
+            nc.vector.tensor_copy(out=t2[:].rearrange("r (p h) -> r p h", h=2),
+                                  in_=t1[:].rearrange("r (h p) -> r p h", h=2))
+
+        def op_BXT():
+            pb = psum.tile([P, P], F32, name="pb", tag="ps")
+            live["pb"] = pb
+            nc.tensor.transpose(pb[:], t2[:], ident[:])
+
+        def op_BX2():
+            nc.vector.tensor_copy(out=bx[:], in_=live["pb"][:, 0:8])
+
+        def op_RD(hh, eng):
+            dst = dgr[hh][:].rearrange("q (j x s t) -> q j x s t", j=4, s=2, t=4)[:, :, :, hh, :]
+            src = draw[hh][:].rearrange("q (j t x) -> q j x t", j=4, t=4)
+            copy_on(eng, dst, src)
+
+        def op_QD(hh):
+            nc.vector.quantize_mx(out=dw[hh][:].bitcast(FP8X4), scales=dsc[hh][:], in_=dgr[hh][:])
+
+        def op_TH(j, hh):
+            words = hraw[j][:].bitcast(F32)
+            tp = psum.tile([P, 2, 2, P], F32, name="tp", tag="ps")
+            live[("tp", j, hh)] = tp
+            for l in range(2):
+                base = 512 * hh + 256 * l
+                for u in range(2):
+                    nc.tensor.transpose(tp[:, l, u, :], words[:, base + u:base + 256:2], ident[:])
+
+        def op_EH(j, hh, eng):
+            dst = hgr[j][:, 1024 * hh:1024 * hh + 1024].bitcast(F32).rearrange(
+                "q (l b u) -> q l b u", l=2, u=2)
+            copy_on(eng, dst, live[("tp", j, hh)][:].rearrange("q l u b -> q l b u"))
+
+        def op_QH(j):
+            nc.vector.quantize_mx(out=hw[j][:].bitcast(FP8X4), scales=hsc[j][:], in_=hgr[j][:])
+
+        def op_S1(j):
+            if j == 0:
+                for c in range(4):
+                    live[("xacc", c)] = psum.tile([P, 4, P], F32, name="xacc%d" % c, tag="ps")
+            for cp in range(2):
+                for l in range(2):
+                    for hh in range(2):
+                        a = (2 * j + cp) * P
+                        b = (2 * hh + l) * P
+                        nc.tensor.matmul_mx(
+                            out=live[("xacc", 2 * l + cp)][:, j, :],
+                            lhsT=dw[hh][:, a:a + P].bitcast(FP8X4), lhsT_scale=dsc[hh][:, a:a + P],
+                            rhs=hw[j][:, b:b + P].bitcast(FP8X4), rhs_scale=hsc[j][:, b:b + P],
+                            start=(hh == 0), stop=(hh == 1))
+
+        def op_EX(c):
+            cp = c % 2
+            nc.vector.tensor_tensor(
+                out=xgr[:, 512 * c:512 * c + 512].rearrange("m (b j) -> m b j", j=4),
+                in0=live[("xacc", c)][:].rearrange("m j b -> m b j"),
+                in1=bx[:, 4 * cp:4 * cp + 4].unsqueeze(1).to_broadcast([P, P, 4]),
+                op=ADD)
+
+        def op_QX():
+            nc.vector.quantize_mx(out=xw[:].bitcast(FP8X4), scales=xsc[:], in_=xgr[:])
+
+        def op_RW(c, k, eng, lo=0, hi=512):
+            if (c, k) not in live:
+                live[(c, k)] = stage.tile([P, 2048], BF16, name="wgr", align_bytes=64)
+            wgr = live[(c, k)]
+            dst = wgr[:, 4 * lo:4 * hi].rearrange("p (c i t) -> p c t i", i=4, t=4)
+            src = wsrc[(c, k)][:, :, lo:hi].rearrange("p t (c i) -> p c t i", i=4)
+            copy_on(eng, dst, src)
+
+        def op_QW(c, k):
+            ww = const.tile([P, 512], U32, name="ww%d_%d" % (c, k), align_bytes=64)
+            wsc = const.tile([P, 512], U8, name="wsc%d_%d" % (c, k), align_bytes=64)
+            live[("ww", c, k)] = (ww, wsc)
+            nc.vector.quantize_mx(out=ww[:].bitcast(FP8X4), scales=wsc[:], in_=live[(c, k)][:])
+
+        def op_MM(c, k):
+            if ("yacc", k) not in live:
+                live[("yacc", k)] = psum.tile([P, 512], F32, name="yacc%d" % k, tag="ps")
+            ww, wsc = live[("ww", c, k)]
+            done = live.get(("n", k), 0)
+            live[("n", k)] = done + 1
+            nc.tensor.matmul_mx(
+                out=live[("yacc", k)][:],
+                lhsT=xw[:, P * c:P * c + P].bitcast(FP8X4), lhsT_scale=xsc[:, P * c:P * c + P],
+                rhs=ww[:].bitcast(FP8X4), rhs_scale=wsc[:],
+                start=(done == 0), stop=(done == 3))
+
+        def op_EY(k):
+            yo = const.tile([P, 512], F32, name="yo%d" % k)
+            nc.vector.tensor_tensor(out=yo[:], in0=live[("yacc", k)][:],
+                                    in1=by[:, 512 * k:512 * k + 512], op=ADD)
+            nc.sync.dma_start(out=ov[:, 512 * k:512 * k + 512], in_=yo[:])
+
+        table = {"BYm": op_BYm, "EBY": op_EBY, "BX1": op_BX1, "BXT": op_BXT, "BX2": op_BX2,
+                 "RD": op_RD, "QD": op_QD, "TH": op_TH, "EH": op_EH, "QH": op_QH, "S1": op_S1,
+                 "EX": op_EX, "QX": op_QX, "RW": op_RW, "QW": op_QW, "MM": op_MM, "EY": op_EY}
+        for item in ORDER:
+            table[item[0]](*item[1:])

@@ -16,7 +16,7 @@ FLOPS = 2 * 2048 * 512 * 128 + 2 * 128 * 2048 * 2048
 
 MANUAL = True
 LOADS = [("h", 0), ("d", 0), ("d", 1), ("h", 1), ("h", 2), ("h", 3), ("w", 0, 0, 1024), ("w", 0, 1024, 1024), ("w", 1, 0, 2048), ("w", 2, 0, 2048), ("w", 3, 0, 1024), ("w", 3, 1024, 512), ("w", 3, 1536, 512)]
-ORDER = [("TH", 0, 0), ("BX1",), ("TH", 0, 1), ("EH", 0, 0, "S"), ("BXT",), ("EH", 0, 1, "S"), ("RD", 0, "V"), ("BYm", 0), ("BYm", 1), ("EBY", 0, "S"), ("RD", 1, "S"), ("BX2",), ("QH", 0), ("QD", 0), ("TH", 1, 0), ("TH", 1, 1), ("TH", 2, 0), ("TH", 2, 1), ("EH", 1, 0, "S"), ("QD", 1), ("TH", 3, 0), ("EH", 1, 1, "S"), ("TH", 3, 1), ("EH", 2, 0, "S"), ("QH", 1), ("S1", 0), ("EH", 3, 0, "S"), ("EH", 2, 1, "V"), ("EH", 3, 1, "S"), ("QH", 2), ("EBY", 1, "S"), ("S1", 1), ("QH", 3), ("RW", 0, 1, "S"), ("RW", 0, 0, "V"), ("S1", 2), ("QW", 0, 0), ("RW", 0, 2, "V"), ("S1", 3), ("RW", 0, 3, "S"), ("QW", 0, 1), ("EX", 0), ("EX", 1), ("EX", 2), ("EX", 3), ("RW", 1, 0, "S"), ("QW", 0, 2), ("QX",), ("QW", 0, 3), ("MM", 0, 0), ("RW", 1, 2, "V"), ("MM", 0, 1), ("MM", 0, 2), ("RW", 1, 1, "S"), ("MM", 0, 3), ("QW", 1, 0), ("QW", 1, 2), ("MM", 1, 0), ("RW", 1, 3, "S"), ("RW", 2, 2, "V"), ("MM", 1, 2), ("QW", 1, 1), ("QW", 2, 2), ("MM", 1, 1), ("RW", 2, 0, "S"), ("QW", 1, 3), ("MM", 2, 2), ("RW", 3, 0, "V"), ("MM", 1, 3), ("RW", 3, 1, "V"), ("RW", 2, 1, "S"), ("QW", 2, 0), ("QW", 3, 0), ("MM", 2, 0), ("QW", 3, 1), ("RW", 2, 3, "S"), ("MM", 3, 0), ("QW", 2, 1), ("MM", 3, 1), ("RW", 3, 2, "V"), ("MM", 2, 1), ("EY", 0), ("RW", 3, 3, "S"), ("QW", 2, 3), ("QW", 3, 2), ("MM", 2, 3), ("EY", 1), ("MM", 3, 2), ("QW", 3, 3), ("EY", 2), ("MM", 3, 3), ("EY", 3)]
+ORDER = [("TH", 0, 0), ("TH", 0, 1), ("EH", 0, 0, "S"), ("EH", 0, 1, "S"), ("RD", 0, "V"), ("RD", 1, "S"), ("QH", 0), ("BX1",), ("QD", 0), ("BXT",), ("TH", 1, 0), ("TH", 1, 1), ("BX2",), ("EH", 1, 0, "V"), ("BYm", 0), ("TH", 2, 0), ("EH", 1, 1, "S"), ("QD", 1), ("TH", 2, 1), ("EH", 2, 0, "S"), ("TH", 3, 0), ("EH", 2, 1, "S"), ("QH", 1), ("TH", 3, 1), ("EH", 3, 0, "S"), ("QH", 2), ("S1", 0), ("EH", 3, 1, "S"), ("EBY", 0, "S"), ("RW", 0, 1, "V"), ("RW", 0, 0, "S"), ("S1", 1), ("QH", 3), ("QW", 0, 1), ("S1", 2), ("RW", 0, 2, "V"), ("RW", 0, 3, "S"), ("S1", 3), ("QW", 0, 0), ("QW", 0, 2), ("BYm", 1), ("EX", 0), ("EBY", 1, "S"), ("EX", 1), ("EX", 2), ("EX", 3), ("RW", 1, 1, "S"), ("QW", 0, 3), ("QX",), ("RW", 1, 0, "V"), ("MM", 0, 0), ("RW", 1, 2, "S"), ("MM", 0, 1), ("MM", 0, 2), ("QW", 1, 1), ("MM", 0, 3), ("QW", 1, 0), ("MM", 1, 1), ("MM", 1, 0), ("RW", 1, 3, "S"), ("RW", 2, 0, "V"), ("QW", 1, 2), ("QW", 2, 0), ("MM", 1, 2), ("RW", 2, 1, "S"), ("QW", 1, 3), ("MM", 2, 0), ("RW", 3, 0, "V"), ("MM", 1, 3), ("RW", 3, 1, "V"), ("RW", 2, 2, "S"), ("QW", 2, 1), ("QW", 3, 0), ("MM", 2, 1), ("QW", 3, 1), ("RW", 2, 3, "S"), ("MM", 3, 0), ("QW", 2, 2), ("MM", 3, 1), ("RW", 3, 3, "V"), ("MM", 2, 2), ("EY", 0), ("RW", 3, 2, "S"), ("QW", 2, 3), ("QW", 3, 3), ("MM", 2, 3), ("EY", 1), ("MM", 3, 3), ("QW", 3, 2), ("EY", 3), ("MM", 3, 2), ("EY", 2)]
 
 
 def tile_model_pb_kernel(tc, h_enc, dec_W, dec_b, map_W, map_b, out):
@@ -31,14 +31,14 @@ def tile_model_pb_kernel(tc, h_enc, dec_W, dec_b, map_W, map_b, out):
         ident = const.tile([P, P], F32, name="ident")
         make_identity(nc, ident[:])
         t1 = const.tile([P, 128], BF16, name="t1")
-        nc.gpsimd.memset(t1[:].bitcast(F32), 0.0)
+        nc.vector.memset(t1[:].bitcast(I32), 0)
         zb = const.tile([P, 2048], BF16, name="zb")
-        nc.gpsimd.memset(zb[:].bitcast(F32), 0.0)
+        nc.vector.memset(zb[:].bitcast(I32), 0)
         dbv = dec_b.rearrange("(h j) (c p) -> c j h p", h=2, c=2)
         for cp in range(2):
-            nc.gpsimd.dma_start(
+            nc.scalar.dma_start(
                 out=t1[4 * cp:4 * cp + 4, :].rearrange("r (h p) -> r h p", h=2), in_=dbv[cp])
-        nc.gpsimd.dma_start(out=zb[0:1, :], in_=map_b.rearrange("(o s) -> o s", o=1))
+        nc.scalar.dma_start(out=zb[0:1, :], in_=map_b.rearrange("(o s) -> o s", o=1))
         ones = const.tile([P, P], BF16, name="ones")
         nc.vector.memset(ones[:], 1.0)
         dgr = [const.tile([P, 4096], BF16, name="dgr%d" % hh, align_bytes=64) for hh in range(2)]

@@ -14,10 +14,6 @@ ADD = mybir.AluOpType.add
 P = 128
 FLOPS = 2 * 2048 * 512 * 128 + 2 * 128 * 2048 * 2048
 
-MANUAL = True
-LOADS = [("h", 0), ("d", 0), ("d", 1), ("h", 1), ("h", 2), ("h", 3), ("w", 0, 0, 1024), ("w", 0, 1024, 1024), ("w", 1, 0, 2048), ("w", 2, 0, 2048), ("w", 3, 0, 1024), ("w", 3, 1024, 512), ("w", 3, 1536, 512)]
-ORDER = [("TH", 0, 0), ("TH", 0, 1), ("EH", 0, 0, "S"), ("EH", 0, 1, "S"), ("RD", 0, "V"), ("RD", 1, "S"), ("QH", 0), ("BX1",), ("QD", 0), ("BXT",), ("TH", 1, 0), ("TH", 1, 1), ("BX2",), ("EH", 1, 0, "V"), ("BYm", 0), ("TH", 2, 0), ("EH", 1, 1, "S"), ("QD", 1), ("TH", 2, 1), ("EH", 2, 0, "S"), ("TH", 3, 0), ("EH", 2, 1, "S"), ("QH", 1), ("TH", 3, 1), ("EH", 3, 0, "S"), ("QH", 2), ("S1", 0), ("EH", 3, 1, "S"), ("EBY", 0, "S"), ("RW", 0, 1, "V"), ("RW", 0, 0, "S"), ("S1", 1), ("QH", 3), ("QW", 0, 1), ("S1", 2), ("RW", 0, 2, "V"), ("RW", 0, 3, "S"), ("S1", 3), ("QW", 0, 0), ("QW", 0, 2), ("BYm", 1), ("EX", 0), ("EBY", 1, "S"), ("EX", 1), ("EX", 2), ("EX", 3), ("RW", 1, 1, "S"), ("QW", 0, 3), ("QX",), ("RW", 1, 0, "V"), ("MM", 0, 0), ("RW", 1, 2, "S"), ("MM", 0, 1), ("MM", 0, 2), ("QW", 1, 1), ("MM", 0, 3), ("QW", 1, 0), ("MM", 1, 1), ("MM", 1, 0), ("RW", 1, 3, "S"), ("RW", 2, 0, "V"), ("QW", 1, 2), ("QW", 2, 0), ("MM", 1, 2), ("RW", 2, 1, "S"), ("QW", 1, 3), ("MM", 2, 0), ("RW", 3, 0, "V"), ("MM", 1, 3), ("RW", 3, 1, "V"), ("RW", 2, 2, "S"), ("QW", 2, 1), ("QW", 3, 0), ("MM", 2, 1), ("QW", 3, 1), ("RW", 2, 3, "S"), ("MM", 3, 0), ("QW", 2, 2), ("MM", 3, 1), ("RW", 3, 3, "V"), ("MM", 2, 2), ("EY", 0), ("RW", 3, 2, "S"), ("QW", 2, 3), ("QW", 3, 3), ("MM", 2, 3), ("EY", 1), ("MM", 3, 3), ("QW", 3, 2), ("EY", 3), ("MM", 3, 2), ("EY", 2)]
-
 
 def tile_model_pb_kernel(tc, h_enc, dec_W, dec_b, map_W, map_b, out):
     nc = tc.nc
@@ -25,52 +21,52 @@ def tile_model_pb_kernel(tc, h_enc, dec_W, dec_b, map_W, map_b, out):
         const = ctx.enter_context(tc.tile_pool(name="const", bufs=1))
         stage = ctx.enter_context(tc.tile_pool(name="stage", bufs=6))
         psum = ctx.enter_context(tc.psum_pool(name="psum", bufs=8))
-        if MANUAL:
-            ctx.enter_context(tc.manual_schedule())
+        ctx.enter_context(tc.manual_schedule())
 
         ident = const.tile([P, P], F32, name="ident")
         make_identity(nc, ident[:])
-        t1 = const.tile([P, 128], BF16, name="t1")
-        nc.vector.memset(t1[:].bitcast(I32), 0)
-        zb = const.tile([P, 2048], BF16, name="zb")
-        nc.vector.memset(zb[:].bitcast(I32), 0)
-        dbv = dec_b.rearrange("(h j) (c p) -> c j h p", h=2, c=2)
-        for cp in range(2):
-            nc.scalar.dma_start(
-                out=t1[4 * cp:4 * cp + 4, :].rearrange("r (h p) -> r h p", h=2), in_=dbv[cp])
-        nc.scalar.dma_start(out=zb[0:1, :], in_=map_b.rearrange("(o s) -> o s", o=1))
         ones = const.tile([P, P], BF16, name="ones")
         nc.vector.memset(ones[:], 1.0)
-        dgr = [const.tile([P, 4096], BF16, name="dgr%d" % hh, align_bytes=64) for hh in range(2)]
-        for hh in range(2):
-            nc.vector.memset(dgr[hh][:].bitcast(I32), 0)
+        brow = const.tile([P, 1024], BF16, name="brow")
+        nc.vector.memset(brow[:].bitcast(I32), 0)
+        scrap = const.tile([P, 1], BF16, name="scrap")
+        nc.scalar.copy(out=scrap[:], in_=ones[:, 0:1])
 
-        hv = h_enc.rearrange("(h j) b c l d -> j (b c) h (l d)", h=2)
-        dv = dec_W.rearrange("(h j) (q t) p -> h q j (t p)", h=2, t=4)
+        hv = h_enc.rearrange("(j e) b c l d -> j (e b c l d)", e=2).rearrange("j (q x) -> j q x", q=P)
+        dv = dec_W.rearrange("(h n) (q t) p -> h q n (t p)", h=2, t=4)
         wv = map_W.rearrange("(c m j) s -> c m j s", m=P, j=4)
-        hraw = [const.tile([P, 2048], BF16, name="hraw%d" % j) for j in range(4)]
         draw = [const.tile([P, 2048], BF16, name="draw%d" % hh) for hh in range(2)]
+        hraw = [const.tile([P, 2048], BF16, name="hraw%d" % j) for j in range(4)]
         wsrc = {}
-        for ld in LOADS:
-            if ld[0] == "h":
-                nc.sync.dma_start(out=hraw[ld[1]][:].rearrange("p (h x) -> p h x", h=2), in_=hv[ld[1]])
-            elif ld[0] == "d":
-                nc.sync.dma_start(out=draw[ld[1]][:].rearrange("p (j x) -> p j x", j=4), in_=dv[ld[1]])
-            else:
-                c, s0, width = ld[1], ld[2], ld[3]
-                wraw = const.tile([P, 4, width], BF16, name="wraw%d_%d" % (c, s0))
-                nc.sync.dma_start(out=wraw[:], in_=wv[c][:, :, s0:s0 + width])
-                for k in range(s0 // 512, (s0 + width) // 512):
-                    wsrc[(c, k)] = wraw[:, :, 512 * k - s0:512 * k - s0 + 512]
 
+        def load_w(c, s0, width):
+            wraw = const.tile([P, 4, width], BF16, name="wraw%d_%d" % (c, s0))
+            nc.sync.dma_start(out=wraw[:], in_=wv[c][:, :, s0:s0 + width])
+            for k in range(s0 // 512, (s0 + width) // 512):
+                wsrc[(c, k)] = wraw[:, :, 512 * k - s0:512 * k - s0 + 512]
+
+        for hh in range(2):
+            nc.sync.dma_start(out=draw[hh][:].rearrange("q (n x) -> q n x", n=4), in_=dv[hh])
+        nc.sync.dma_start(out=brow[0:1, :], in_=dec_b.rearrange("(o n) p -> o (n p)", o=1))
+        load_w(0, 0, 1024)
+        for j in range(4):
+            nc.sync.dma_start(out=hraw[j][:], in_=hv[j])
+        load_w(0, 1024, 1024)
+        load_w(1, 0, 1024)
+        load_w(1, 1024, 1024)
+        load_w(2, 0, 2048)
+        load_w(3, 0, 2048)
         by = const.tile([P, 2048], BF16, name="by")
-        t2 = const.tile([P, 128], F32, name="t2")
-        bx = const.tile([P, 8], F32, name="bx")
-        dw = [const.tile([P, 1024], U32, name="dw%d" % hh, align_bytes=64) for hh in range(2)]
-        dsc = [const.tile([P, 1024], U8, name="dsc%d" % hh, align_bytes=64) for hh in range(2)]
+        nc.sync.dma_start(out=by[:], in_=map_b.partition_broadcast(P))
+
+        decb = const.tile([P, 1024], BF16, name="decb")
+        dgr = [const.tile([P, 2048], BF16, name="dgr%d" % hh, align_bytes=64) for hh in range(2)]
+        dw = [const.tile([P, 512], U32, name="dw%d" % hh, align_bytes=64) for hh in range(2)]
+        dsc = [const.tile([P, 512], U8, name="dsc%d" % hh, align_bytes=64) for hh in range(2)]
+        hgr = [const.tile([P, 2048], BF16, name="hgr%d" % j, align_bytes=64) for j in range(4)]
         hw = [const.tile([P, 512], U32, name="hw%d" % j, align_bytes=64) for j in range(4)]
         hsc = [const.tile([P, 512], U8, name="hsc%d" % j, align_bytes=64) for j in range(4)]
-        hgr = [const.tile([P, 2048], BF16, name="hgr%d" % j, align_bytes=64) for j in range(4)]
+        xrec = const.tile([P, 2048], BF16, name="xrec", align_bytes=64)
         xgr = const.tile([P, 2048], BF16, name="xgr", align_bytes=64)
         xw = const.tile([P, 512], U32, name="xw", align_bytes=64)
         xsc = const.tile([P, 512], U8, name="xsc", align_bytes=64)
@@ -83,114 +79,174 @@ def tile_model_pb_kernel(tc, h_enc, dec_W, dec_b, map_W, map_b, out):
             else:
                 nc.scalar.copy(out=dst, in_=src)
 
-        def op_BYm(g):
-            pby = psum.tile([P, 1024], BF16, name="pby", tag="ps")
-            live[("pby", g)] = pby
+        def BB():
+            pb = psum.tile([P, 1024], BF16, name="pb", tag="ps")
             for e in range(2):
-                nc.tensor.matmul(out=pby[:, 512 * e:512 * e + 512], lhsT=ones[:],
-                                 rhs=zb[:, 1024 * g + 512 * e:1024 * g + 512 * e + 512],
-                                 start=True, stop=True)
+                nc.tensor.matmul(out=pb[:, 512 * e:512 * e + 512], lhsT=ones[:],
+                                 rhs=brow[:, 512 * e:512 * e + 512], start=True, stop=True)
+            nc.scalar.copy(out=decb[:].rearrange("b (p n) -> b p n", n=8),
+                           in_=pb[:].rearrange("b (n p) -> b p n", n=8))
 
-        def op_EBY(g, eng):
-            copy_on(eng, by[:, 1024 * g:1024 * g + 1024], live[("pby", g)][:])
+        def RD(hh):
+            nc.vector.tensor_copy(
+                out=dgr[hh][:].rearrange("q (n c i t) -> q n c t i", n=4, i=4, t=4),
+                in_=draw[hh][:].rearrange("q (n t c i) -> q n c t i", n=4, t=4, i=4))
 
-        def op_BX1():
-            nc.vector.tensor_copy(out=t2[:].rearrange("r (p h) -> r p h", h=2),
-                                  in_=t1[:].rearrange("r (h p) -> r p h", h=2))
-
-        def op_BXT():
-            pb = psum.tile([P, P], F32, name="pb", tag="ps")
-            live["pb"] = pb
-            nc.tensor.transpose(pb[:], t2[:], ident[:])
-
-        def op_BX2():
-            nc.vector.tensor_copy(out=bx[:], in_=live["pb"][:, 0:8])
-
-        def op_RD(hh, eng):
-            dst = dgr[hh][:].rearrange("q (j x s t) -> q j x s t", j=4, s=2, t=4)[:, :, :, hh, :]
-            src = draw[hh][:].rearrange("q (j t x) -> q j x t", j=4, t=4)
-            copy_on(eng, dst, src)
-
-        def op_QD(hh):
+        def QD(hh):
             nc.vector.quantize_mx(out=dw[hh][:].bitcast(FP8X4), scales=dsc[hh][:], in_=dgr[hh][:])
 
-        def op_TH(j, hh):
+        def TH(j):
             words = hraw[j][:].bitcast(F32)
-            tp = psum.tile([P, 2, 2, P], F32, name="tp", tag="ps")
-            live[("tp", j, hh)] = tp
             for l in range(2):
-                base = 512 * hh + 256 * l
-                for u in range(2):
-                    nc.tensor.transpose(tp[:, l, u, :], words[:, base + u:base + 256:2], ident[:])
+                tp = psum.tile([P, 2, 2, P], F32, name="tp", tag="ps")
+                live[("tp", j, l)] = tp
+                for w in range(2):
+                    base = 512 * w + 256 * l
+                    for u in range(2):
+                        nc.tensor.transpose(tp[:, w, u, :], words[:, base + u:base + 256:2], ident[:])
 
-        def op_EH(j, hh, eng):
-            dst = hgr[j][:, 1024 * hh:1024 * hh + 1024].bitcast(F32).rearrange(
-                "q (l b u) -> q l b u", l=2, u=2)
-            copy_on(eng, dst, live[("tp", j, hh)][:].rearrange("q l u b -> q l b u"))
+        def EH(j):
+            for l in range(2):
+                nc.scalar.copy(
+                    out=hgr[j][:, 1024 * l:1024 * l + 1024].bitcast(F32).rearrange("q (r v) -> q r v", v=4),
+                    in_=live[("tp", j, l)][:].rearrange("q w u r -> q r (w u)"))
 
-        def op_QH(j):
+        def QH(j):
             nc.vector.quantize_mx(out=hw[j][:].bitcast(FP8X4), scales=hsc[j][:], in_=hgr[j][:])
 
-        def op_S1(j):
-            if j == 0:
-                for c in range(4):
-                    live[("xacc", c)] = psum.tile([P, 4, P], F32, name="xacc%d" % c, tag="ps")
-            for cp in range(2):
-                for l in range(2):
-                    for hh in range(2):
-                        a = (2 * j + cp) * P
-                        b = (2 * hh + l) * P
-                        nc.tensor.matmul_mx(
-                            out=live[("xacc", 2 * l + cp)][:, j, :],
-                            lhsT=dw[hh][:, a:a + P].bitcast(FP8X4), lhsT_scale=dsc[hh][:, a:a + P],
-                            rhs=hw[j][:, b:b + P].bitcast(FP8X4), rhs_scale=hsc[j][:, b:b + P],
-                            start=(hh == 0), stop=(hh == 1))
+        def S1(j):
+            for g in range(4):
+                if j == 0:
+                    live[("xb", g)] = psum.tile([P, 8, 64], F32, name="xb%d" % g, tag="ps")
+                l, pc = g // 2, g % 2
+                for e in range(2):
+                    n = 2 * j + e
+                    a = 256 * l + 128 * e
+                    b = 128 * (n % 4) + 64 * pc
+                    nc.tensor.matmul_mx(
+                        out=live[("xb", g)][:, n, :],
+                        lhsT=hw[j][:, a:a + P].bitcast(FP8X4), lhsT_scale=hsc[j][:, a:a + P],
+                        rhs=dw[n // 4][:, b:b + 64].bitcast(FP8X4), rhs_scale=dsc[n // 4][:, b:b + 64],
+                        start=True, stop=True)
 
-        def op_EX(c):
-            cp = c % 2
+        def EX(g):
             nc.vector.tensor_tensor(
-                out=xgr[:, 512 * c:512 * c + 512].rearrange("m (b j) -> m b j", j=4),
-                in0=live[("xacc", c)][:].rearrange("m j b -> m b j"),
-                in1=bx[:, 4 * cp:4 * cp + 4].unsqueeze(1).to_broadcast([P, P, 4]),
+                out=xrec[:, 512 * g:512 * g + 512].rearrange("b (p n) -> b p n", n=8),
+                in0=live[("xb", g)][:].rearrange("b n p -> b p n"),
+                in1=decb[:, 512 * (g % 2):512 * (g % 2) + 512].rearrange("b (p n) -> b p n", n=8),
                 op=ADD)
 
-        def op_QX():
-            nc.vector.quantize_mx(out=xw[:].bitcast(FP8X4), scales=xsc[:], in_=xgr[:])
+        def TX(i):
+            words = xrec[:].bitcast(F32)
+            xt = psum.tile([P, 2, 2, P], F32, name="xt", tag="ps")
+            live[("xt", i)] = xt
+            for c in range(2):
+                base = 512 * i + 256 * c
+                for u in range(2):
+                    nc.tensor.transpose(xt[:, c, u, :], words[:, base + u:base + 256:2], ident[:])
 
-        def op_RW(c, k, eng, lo=0, hi=512):
+        def EXT(i):
+            nc.scalar.copy(
+                out=xgr[:, 1024 * i:1024 * i + 1024].bitcast(F32).rearrange("q (c b u) -> q c b u", c=2, u=2),
+                in_=live[("xt", i)][:].rearrange("q c u b -> q c b u"))
+
+        def QX(i):
+            nc.vector.quantize_mx(out=xw[:, 256 * i:256 * i + 256].bitcast(FP8X4),
+                                  scales=xsc[:, 256 * i:256 * i + 256],
+                                  in_=xgr[:, 1024 * i:1024 * i + 1024])
+
+        def RW(eng, c, k, lo=0, hi=512):
             if (c, k) not in live:
                 live[(c, k)] = stage.tile([P, 2048], BF16, name="wgr", align_bytes=64)
-            wgr = live[(c, k)]
-            dst = wgr[:, 4 * lo:4 * hi].rearrange("p (c i t) -> p c t i", i=4, t=4)
+            dst = live[(c, k)][:, 4 * lo:4 * hi].rearrange("p (c i t) -> p c t i", i=4, t=4)
             src = wsrc[(c, k)][:, :, lo:hi].rearrange("p t (c i) -> p c t i", i=4)
             copy_on(eng, dst, src)
 
-        def op_QW(c, k):
+        def QW(c, k):
             ww = const.tile([P, 512], U32, name="ww%d_%d" % (c, k), align_bytes=64)
             wsc = const.tile([P, 512], U8, name="wsc%d_%d" % (c, k), align_bytes=64)
             live[("ww", c, k)] = (ww, wsc)
             nc.vector.quantize_mx(out=ww[:].bitcast(FP8X4), scales=wsc[:], in_=live[(c, k)][:])
 
-        def op_MM(c, k):
-            if ("yacc", k) not in live:
+        def MM(c, k):
+            if c == 0:
                 live[("yacc", k)] = psum.tile([P, 512], F32, name="yacc%d" % k, tag="ps")
             ww, wsc = live[("ww", c, k)]
-            done = live.get(("n", k), 0)
-            live[("n", k)] = done + 1
             nc.tensor.matmul_mx(
                 out=live[("yacc", k)][:],
                 lhsT=xw[:, P * c:P * c + P].bitcast(FP8X4), lhsT_scale=xsc[:, P * c:P * c + P],
                 rhs=ww[:].bitcast(FP8X4), rhs_scale=wsc[:],
-                start=(done == 0), stop=(done == 3))
+                start=(c == 0), stop=(c == 3))
 
-        def op_EY(k):
+        def EY(k):
             yo = const.tile([P, 512], F32, name="yo%d" % k)
             nc.vector.tensor_tensor(out=yo[:], in0=live[("yacc", k)][:],
                                     in1=by[:, 512 * k:512 * k + 512], op=ADD)
             nc.sync.dma_start(out=ov[:, 512 * k:512 * k + 512], in_=yo[:])
 
-        table = {"BYm": op_BYm, "EBY": op_EBY, "BX1": op_BX1, "BXT": op_BXT, "BX2": op_BX2,
-                 "RD": op_RD, "QD": op_QD, "TH": op_TH, "EH": op_EH, "QH": op_QH, "S1": op_S1,
-                 "EX": op_EX, "QX": op_QX, "RW": op_RW, "QW": op_QW, "MM": op_MM, "EY": op_EY}
-        for item in ORDER:
-            table[item[0]](*item[1:])
+        BB()
+        RD(0)
+        RD(1)
+        QD(0)
+        QD(1)
+        RW("V", 0, 0)
+        RW("S", 0, 1)
+        TH(0)
+        TH(1)
+        EH(0)
+        QW(0, 0)
+        TH(2)
+        QH(0)
+        S1(0)
+        EH(1)
+        QW(0, 1)
+        TH(3)
+        QH(1)
+        S1(1)
+        EH(2)
+        QH(2)
+        S1(2)
+        EH(3)
+        QH(3)
+        S1(3)
+
+        RW("S", 0, 2)
+        RW("S", 1, 0)
+        for g in range(4):
+            EX(g)
+            if g % 2:
+                TX(g // 2)
+        EXT(0)
+        RW("V", 0, 3)
+        EXT(1)
+        QW(0, 2)
+        QX(0)
+        QW(0, 3)
+        QX(1)
+        MM(0, 0)
+        MM(0, 1)
+        MM(0, 2)
+        MM(0, 3)
+        units = [(c, k) for c in range(1, 4) for k in range(0, 4, 2)]
+        for i, (c, k) in enumerate(units):
+            if i > 0:
+                RW("S", c, k)
+            if i < 5:
+                RW("V", c, k + 1)
+            else:
+                RW("S", c, k + 1)
+            if i > 0:
+                pc, pk = units[i - 1]
+                QW(pc, pk)
+                MM(pc, pk)
+            if i < 5:
+                QW(c, k + 1)
+                MM(c, k + 1)
+        EY(1)
+        QW(3, 2)
+        MM(3, 2)
+        EY(0)
+        QW(3, 3)
+        MM(3, 3)
+        EY(2)
+        EY(3)

@@ -27,7 +27,7 @@ def tile_model_pb_kernel(tc, h_enc, dec_W, dec_b, map_W, map_b, out):
         make_identity(nc, ident[:])
         ones = const.tile([P, P], BF16, name="ones")
         nc.vector.memset(ones[:], 1.0)
-        brow = const.tile([P, 1024], BF16, name="brow")
+        brow = const.tile([P, 3072], BF16, name="brow")
         nc.vector.memset(brow[:].bitcast(I32), 0)
         scrap = const.tile([P, 1], BF16, name="scrap")
         nc.scalar.copy(out=scrap[:], in_=ones[:, 0:1])
@@ -45,19 +45,22 @@ def tile_model_pb_kernel(tc, h_enc, dec_W, dec_b, map_W, map_b, out):
             for k in range(s0 // 512, (s0 + width) // 512):
                 wsrc[(c, k)] = wraw[:, :, 512 * k - s0:512 * k - s0 + 512]
 
-        for hh in range(2):
-            nc.sync.dma_start(out=draw[hh][:].rearrange("q (n x) -> q n x", n=4), in_=dv[hh])
-        nc.sync.dma_start(out=brow[0:1, :], in_=dec_b.rearrange("(o n) p -> o (n p)", o=1))
+        nc.sync.dma_start(out=draw[0][:].rearrange("q (n x) -> q n x", n=4), in_=dv[0])
+        nc.sync.dma_start(out=brow[0:1, 0:1024], in_=dec_b.rearrange("(o n) p -> o (n p)", o=1))
+        nc.sync.dma_start(out=brow[0:1, 1024:3072], in_=map_b.rearrange("(o s) -> o s", o=1))
+        nc.sync.dma_start(out=draw[1][:].rearrange("q (n x) -> q n x", n=4), in_=dv[1])
         load_w(0, 0, 1024)
         for j in range(4):
             nc.sync.dma_start(out=hraw[j][:], in_=hv[j])
         load_w(0, 1024, 1024)
         load_w(1, 0, 1024)
         load_w(1, 1024, 1024)
-        load_w(2, 0, 2048)
-        load_w(3, 0, 2048)
+        load_w(2, 0, 1024)
+        load_w(2, 1024, 1024)
+        load_w(3, 0, 1024)
+        load_w(3, 1024, 512)
+        load_w(3, 1536, 512)
         by = const.tile([P, 2048], BF16, name="by")
-        nc.sync.dma_start(out=by[:], in_=map_b.partition_broadcast(P))
 
         decb = const.tile([P, 1024], BF16, name="decb")
         dgr = [const.tile([P, 2048], BF16, name="dgr%d" % hh, align_bytes=64) for hh in range(2)]
@@ -79,13 +82,17 @@ def tile_model_pb_kernel(tc, h_enc, dec_W, dec_b, map_W, map_b, out):
             else:
                 nc.scalar.copy(out=dst, in_=src)
 
-        def BB():
+        def spread(g):
             pb = psum.tile([P, 1024], BF16, name="pb", tag="ps")
             for e in range(2):
                 nc.tensor.matmul(out=pb[:, 512 * e:512 * e + 512], lhsT=ones[:],
-                                 rhs=brow[:, 512 * e:512 * e + 512], start=True, stop=True)
-            nc.scalar.copy(out=decb[:].rearrange("b (p n) -> b p n", n=8),
-                           in_=pb[:].rearrange("b (n p) -> b p n", n=8))
+                                 rhs=brow[:, 1024 * g + 512 * e:1024 * g + 512 * e + 512],
+                                 start=True, stop=True)
+            if g == 0:
+                nc.scalar.copy(out=decb[:].rearrange("b (p n) -> b p n", n=8),
+                               in_=pb[:].rearrange("b (n p) -> b p n", n=8))
+            else:
+                nc.scalar.copy(out=by[:, 1024 * g - 1024:1024 * g], in_=pb[:])
 
         def RD(hh):
             nc.vector.tensor_copy(
@@ -184,7 +191,9 @@ def tile_model_pb_kernel(tc, h_enc, dec_W, dec_b, map_W, map_b, out):
                                     in1=by[:, 512 * k:512 * k + 512], op=ADD)
             nc.sync.dma_start(out=ov[:, 512 * k:512 * k + 512], in_=yo[:])
 
-        BB()
+        spread(0)
+        spread(1)
+        spread(2)
         RD(0)
         RD(1)
         QD(0)

@@ -19,8 +19,9 @@ def tile_model_pb_kernel(tc, h_enc, dec_W, dec_b, map_W, map_b, out):
     nc = tc.nc
     with ExitStack() as ctx:
         const = ctx.enter_context(tc.tile_pool(name="const", bufs=1))
-        stage = ctx.enter_context(tc.tile_pool(name="stage", bufs=6))
-        psum = ctx.enter_context(tc.psum_pool(name="psum", bufs=8))
+        stage = ctx.enter_context(tc.tile_pool(name="stage", bufs=4))
+        psum = ctx.enter_context(tc.psum_pool(name="psum", bufs=4))
+        accs = ctx.enter_context(tc.psum_pool(name="accs", bufs=1))
         ctx.enter_context(tc.manual_schedule())
 
         ident = const.tile([P, P], F32, name="ident")
@@ -45,21 +46,30 @@ def tile_model_pb_kernel(tc, h_enc, dec_W, dec_b, map_W, map_b, out):
             for k in range(s0 // 512, (s0 + width) // 512):
                 wsrc[(c, k)] = wraw[:, :, 512 * k - s0:512 * k - s0 + 512]
 
-        nc.sync.dma_start(out=draw[0][:].rearrange("q (n x) -> q n x", n=4), in_=dv[0])
-        nc.sync.dma_start(out=brow[0:1, 0:1024], in_=dec_b.rearrange("(o n) p -> o (n p)", o=1))
-        nc.sync.dma_start(out=brow[0:1, 1024:3072], in_=map_b.rearrange("(o s) -> o s", o=1))
-        nc.sync.dma_start(out=draw[1][:].rearrange("q (n x) -> q n x", n=4), in_=dv[1])
-        load_w(0, 0, 1024)
-        for j in range(4):
+        def load_d(hh):
+            nc.sync.dma_start(out=draw[hh][:].rearrange("q (n x) -> q n x", n=4), in_=dv[hh])
+
+        def load_h(j):
             nc.sync.dma_start(out=hraw[j][:], in_=hv[j])
+
+        def load_b():
+            nc.sync.dma_start(out=brow[0:1, 0:1024], in_=dec_b.rearrange("(o n) p -> o (n p)", o=1))
+            nc.sync.dma_start(out=brow[0:1, 1024:3072], in_=map_b.rearrange("(o s) -> o s", o=1))
+
+        load_h(0)
+        load_b()
+        load_d(0)
+        load_d(1)
+        load_h(1)
+        load_h(2)
+        load_h(3)
+        load_w(0, 0, 1024)
         load_w(0, 1024, 1024)
-        load_w(1, 0, 1024)
-        load_w(1, 1024, 1024)
+        load_w(1, 0, 2048)
         load_w(2, 0, 1024)
         load_w(2, 1024, 1024)
         load_w(3, 0, 1024)
-        load_w(3, 1024, 512)
-        load_w(3, 1536, 512)
+        load_w(3, 1024, 1024)
         by = const.tile([P, 2048], BF16, name="by")
 
         decb = const.tile([P, 1024], BF16, name="decb")
@@ -82,17 +92,25 @@ def tile_model_pb_kernel(tc, h_enc, dec_W, dec_b, map_W, map_b, out):
             else:
                 nc.scalar.copy(out=dst, in_=src)
 
-        def spread(g):
+        def SPM(g):
             pb = psum.tile([P, 1024], BF16, name="pb", tag="ps")
             for e in range(2):
                 nc.tensor.matmul(out=pb[:, 512 * e:512 * e + 512], lhsT=ones[:],
                                  rhs=brow[:, 1024 * g + 512 * e:1024 * g + 512 * e + 512],
                                  start=True, stop=True)
+            live[("pb", g)] = pb
+
+        def SPC(g):
+            pb = live[("pb", g)]
             if g == 0:
                 nc.scalar.copy(out=decb[:].rearrange("b (p n) -> b p n", n=8),
                                in_=pb[:].rearrange("b (n p) -> b p n", n=8))
             else:
                 nc.scalar.copy(out=by[:, 1024 * g - 1024:1024 * g], in_=pb[:])
+
+        def spread(g):
+            SPM(g)
+            SPC(g)
 
         def RD(hh):
             nc.vector.tensor_copy(
@@ -102,21 +120,26 @@ def tile_model_pb_kernel(tc, h_enc, dec_W, dec_b, map_W, map_b, out):
         def QD(hh):
             nc.vector.quantize_mx(out=dw[hh][:].bitcast(FP8X4), scales=dsc[hh][:], in_=dgr[hh][:])
 
-        def TH(j):
+        def TH1(j, l):
             words = hraw[j][:].bitcast(F32)
-            for l in range(2):
-                tp = psum.tile([P, 2, 2, P], F32, name="tp", tag="ps")
-                live[("tp", j, l)] = tp
-                for w in range(2):
-                    base = 512 * w + 256 * l
-                    for u in range(2):
-                        nc.tensor.transpose(tp[:, w, u, :], words[:, base + u:base + 256:2], ident[:])
+            tp = psum.tile([P, 2, 2, P], F32, name="tp", tag="ps")
+            live[("tp", j, l)] = tp
+            for w in range(2):
+                base = 512 * w + 256 * l
+                for u in range(2):
+                    nc.tensor.transpose(tp[:, w, u, :], words[:, base + u:base + 256:2], ident[:])
+
+        def TH(j):
+            TH1(j, 0)
+            TH1(j, 1)
+
+        def EH1(eng, j, l):
+            copy_on(eng, hgr[j][:, 1024 * l:1024 * l + 1024].bitcast(F32).rearrange("q (r v) -> q r v", v=4),
+                    live[("tp", j, l)][:].rearrange("q w u r -> q r (w u)"))
 
         def EH(j):
-            for l in range(2):
-                nc.scalar.copy(
-                    out=hgr[j][:, 1024 * l:1024 * l + 1024].bitcast(F32).rearrange("q (r v) -> q r v", v=4),
-                    in_=live[("tp", j, l)][:].rearrange("q w u r -> q r (w u)"))
+            EH1("S", j, 0)
+            EH1("S", j, 1)
 
         def QH(j):
             nc.vector.quantize_mx(out=hw[j][:].bitcast(FP8X4), scales=hsc[j][:], in_=hgr[j][:])
@@ -124,7 +147,7 @@ def tile_model_pb_kernel(tc, h_enc, dec_W, dec_b, map_W, map_b, out):
         def S1(j):
             for g in range(4):
                 if j == 0:
-                    live[("xb", g)] = psum.tile([P, 8, 64], F32, name="xb%d" % g, tag="ps")
+                    live[("xb", g)] = accs.tile([P, 8, 64], F32, name="xb%d" % g, tag="acc%d" % g)
                 l, pc = g // 2, g % 2
                 for e in range(2):
                     n = 2 * j + e
@@ -143,14 +166,18 @@ def tile_model_pb_kernel(tc, h_enc, dec_W, dec_b, map_W, map_b, out):
                 in1=decb[:, 512 * (g % 2):512 * (g % 2) + 512].rearrange("b (p n) -> b p n", n=8),
                 op=ADD)
 
-        def TX(i):
+        def TX1(g):
             words = xrec[:].bitcast(F32)
-            xt = psum.tile([P, 2, 2, P], F32, name="xt", tag="ps")
-            live[("xt", i)] = xt
-            for c in range(2):
-                base = 512 * i + 256 * c
-                for u in range(2):
-                    nc.tensor.transpose(xt[:, c, u, :], words[:, base + u:base + 256:2], ident[:])
+            i, c = g // 2, g % 2
+            if ("xt", i) not in live:
+                live[("xt", i)] = psum.tile([P, 2, 2, P], F32, name="xt", tag="ps")
+            base = 256 * g
+            for u in range(2):
+                nc.tensor.transpose(live[("xt", i)][:, c, u, :], words[:, base + u:base + 256:2], ident[:])
+
+        def TX(i):
+            TX1(2 * i)
+            TX1(2 * i + 1)
 
         def EXT(i):
             nc.scalar.copy(
@@ -163,27 +190,38 @@ def tile_model_pb_kernel(tc, h_enc, dec_W, dec_b, map_W, map_b, out):
                                   in_=xgr[:, 1024 * i:1024 * i + 1024])
 
         def RW(eng, c, k, lo=0, hi=512):
-            if (c, k) not in live:
-                live[(c, k)] = stage.tile([P, 2048], BF16, name="wgr", align_bytes=64)
-            dst = live[(c, k)][:, 4 * lo:4 * hi].rearrange("p (c i t) -> p c t i", i=4, t=4)
+            if (c, k // 2) not in live:
+                live[(c, k // 2)] = stage.tile([P, 4096], BF16, name="wgr", align_bytes=64)
+            base = 512 * (k % 2)
+            dst = live[(c, k // 2)][:, 4 * (base + lo):4 * (base + hi)].rearrange("p (c i t) -> p c t i", i=4, t=4)
             src = wsrc[(c, k)][:, :, lo:hi].rearrange("p t (c i) -> p c t i", i=4)
             copy_on(eng, dst, src)
+
+        def QP(c, g):
+            ww = const.tile([P, 1024], U32, name="wwp%d_%d" % (c, g), align_bytes=64)
+            wsc = const.tile([P, 1024], U8, name="wscp%d_%d" % (c, g), align_bytes=64)
+            for e in range(2):
+                live[("ww", c, 2 * g + e)] = (ww[:, 512 * e:512 * e + 512], wsc[:, 512 * e:512 * e + 512])
+            nc.vector.quantize_mx(out=ww[:].bitcast(FP8X4), scales=wsc[:], in_=live[(c, g)][:])
 
         def QW(c, k):
             ww = const.tile([P, 512], U32, name="ww%d_%d" % (c, k), align_bytes=64)
             wsc = const.tile([P, 512], U8, name="wsc%d_%d" % (c, k), align_bytes=64)
-            live[("ww", c, k)] = (ww, wsc)
-            nc.vector.quantize_mx(out=ww[:].bitcast(FP8X4), scales=wsc[:], in_=live[(c, k)][:])
+            live[("ww", c, k)] = (ww[:], wsc[:])
+            nc.vector.quantize_mx(out=ww[:].bitcast(FP8X4), scales=wsc[:],
+                                  in_=live[(c, k // 2)][:, 2048 * (k % 2):2048 * (k % 2) + 2048])
 
         def MM(c, k):
-            if c == 0:
-                live[("yacc", k)] = psum.tile([P, 512], F32, name="yacc%d" % k, tag="ps")
+            cnt = live.get(("n", k), 0)
+            live[("n", k)] = cnt + 1
+            if cnt == 0:
+                live[("yacc", k)] = accs.tile([P, 512], F32, name="yacc%d" % k, tag="acc%d" % k)
             ww, wsc = live[("ww", c, k)]
             nc.tensor.matmul_mx(
                 out=live[("yacc", k)][:],
                 lhsT=xw[:, P * c:P * c + P].bitcast(FP8X4), lhsT_scale=xsc[:, P * c:P * c + P],
-                rhs=ww[:].bitcast(FP8X4), rhs_scale=wsc[:],
-                start=(c == 0), stop=(c == 3))
+                rhs=ww.bitcast(FP8X4), rhs_scale=wsc,
+                start=(cnt == 0), stop=(cnt == 3))
 
         def EY(k):
             yo = const.tile([P, 512], F32, name="yo%d" % k)
@@ -191,71 +229,64 @@ def tile_model_pb_kernel(tc, h_enc, dec_W, dec_b, map_W, map_b, out):
                                     in1=by[:, 512 * k:512 * k + 512], op=ADD)
             nc.sync.dma_start(out=ov[:, 512 * k:512 * k + 512], in_=yo[:])
 
+        TH(0)
+        EH(0)
+        RD(0)
         spread(0)
         spread(1)
         spread(2)
-        RD(0)
-        RD(1)
-        QD(0)
-        QD(1)
-        RW("V", 0, 0)
-        RW("S", 0, 1)
-        TH(0)
-        TH(1)
-        EH(0)
-        QW(0, 0)
-        TH(2)
         QH(0)
+        QD(0)
+        RD(1)
         S1(0)
-        EH(1)
-        QW(0, 1)
-        TH(3)
+        TH(1)
+        QD(1)
+        EH1("V", 1, 0)
+        EH1("S", 1, 1)
+        TH(2)
+        EH1("S", 2, 0)
+        EH1("S", 2, 1)
         QH(1)
+        TH(3)
+        EH1("V", 3, 0)
+        EH1("S", 3, 1)
         S1(1)
-        EH(2)
         QH(2)
-        S1(2)
-        EH(3)
         QH(3)
+        S1(2)
         S1(3)
-
-        RW("S", 0, 2)
-        RW("S", 1, 0)
+        RW("S", 0, 0)
+        RW("V", 0, 1)
         for g in range(4):
             EX(g)
-            if g % 2:
-                TX(g // 2)
+            TX1(g)
+        RW("S", 0, 2)
+        QP(0, 0)
         EXT(0)
-        RW("V", 0, 3)
         EXT(1)
-        QW(0, 2)
+        RW("V", 0, 3)
         QX(0)
-        QW(0, 3)
         QX(1)
-        MM(0, 0)
-        MM(0, 1)
-        MM(0, 2)
-        MM(0, 3)
-        units = [(c, k) for c in range(1, 4) for k in range(0, 4, 2)]
-        for i, (c, k) in enumerate(units):
-            if i > 0:
-                RW("S", c, k)
-            if i < 5:
-                RW("V", c, k + 1)
-            else:
-                RW("S", c, k + 1)
-            if i > 0:
-                pc, pk = units[i - 1]
-                QW(pc, pk)
-                MM(pc, pk)
-            if i < 5:
-                QW(c, k + 1)
-                MM(c, k + 1)
-        EY(1)
-        QW(3, 2)
+        for k in range(2):
+            MM(0, k)
+        RW("S", 1, 0)
+        QP(0, 1)
+        for k in range(2, 4):
+            MM(0, k)
+        RW("V", 1, 1)
+        pairs = [(c, g) for c in range(1, 4) for g in range(2)]
+        for i in range(1, 6):
+            c, g = pairs[i]
+            RW("S", c, 2 * g)
+            RW("V", c, 2 * g + 1)
+            c, g = pairs[i - 1]
+            QP(c, g)
+            MM(c, 2 * g)
+            MM(c, 2 * g + 1)
+        QP(3, 1)
         MM(3, 2)
-        EY(0)
-        QW(3, 3)
         MM(3, 3)
+        EY(0)
+        EY(1)
         EY(2)
         EY(3)

@@ -275,7 +275,7 @@ def tile_model_pb_kernel(tc, h_enc, dec_W, dec_b, map_W, map_b, out):
             MM(0, k)
         RW("V", 1, 1)
         pairs = [(c, g) for c in range(1, 4) for g in range(2)]
-        for i in range(1, 6):
+        for i in range(1, 5):
             c, g = pairs[i]
             RW("S", c, 2 * g)
             RW("V", c, 2 * g + 1)
@@ -283,10 +283,17 @@ def tile_model_pb_kernel(tc, h_enc, dec_W, dec_b, map_W, map_b, out):
             QP(c, g)
             MM(c, 2 * g)
             MM(c, 2 * g + 1)
-        QP(3, 1)
-        MM(3, 2)
+        RW("S", 3, 2)
+        QW(3, 1)
+        MM(3, 1)
+        RW("V", 3, 3)
+        QW(3, 0)
+        MM(3, 0)
+        QW(3, 3)
         MM(3, 3)
-        EY(0)
         EY(1)
-        EY(2)
+        EY(0)
+        QW(3, 2)
+        MM(3, 2)
         EY(3)
+        EY(2)

from contextlib import ExitStack

import concourse.mybir as mybir
from concourse.masks import make_identity

F32 = mybir.dt.float32
BF16 = mybir.dt.bfloat16
U32 = mybir.dt.uint32
U8 = mybir.dt.uint8
I32 = mybir.dt.int32
FP8X4 = mybir.dt.float8_e4m3fn_x4
ADD = mybir.AluOpType.add

P = 128
FLOPS = 2 * 2048 * 512 * 128 + 2 * 128 * 2048 * 2048


def tile_model_pb_kernel(tc, h_enc, dec_W, dec_b, map_W, map_b, out):
    nc = tc.nc
    with ExitStack() as ctx:
        const = ctx.enter_context(tc.tile_pool(name="const", bufs=1))
        stage = ctx.enter_context(tc.tile_pool(name="stage", bufs=4))
        psum = ctx.enter_context(tc.psum_pool(name="psum", bufs=4))
        accs = ctx.enter_context(tc.psum_pool(name="accs", bufs=1))
        ctx.enter_context(tc.manual_schedule())

        ident = const.tile([P, P], F32, name="ident")
        make_identity(nc, ident[:])
        ones = const.tile([P, P], BF16, name="ones")
        nc.vector.memset(ones[:], 1.0)
        brow = const.tile([P, 3072], BF16, name="brow")
        nc.vector.memset(brow[:].bitcast(I32), 0)
        scrap = const.tile([P, 1], BF16, name="scrap")
        nc.scalar.copy(out=scrap[:], in_=ones[:, 0:1])

        hv = h_enc.rearrange("(j e) b c l d -> j (e b c l d)", e=2).rearrange("j (q x) -> j q x", q=P)
        dv = dec_W.rearrange("(h n) (q t) p -> h q n (t p)", h=2, t=4)
        wv = map_W.rearrange("(c m j) s -> c m j s", m=P, j=4)
        draw = [const.tile([P, 2048], BF16, name="draw%d" % hh) for hh in range(2)]
        hraw = [const.tile([P, 2048], BF16, name="hraw%d" % j) for j in range(4)]
        wsrc = {}

        def load_w(c, s0, width):
            wraw = const.tile([P, 4, width], BF16, name="wraw%d_%d" % (c, s0))
            nc.sync.dma_start(out=wraw[:], in_=wv[c][:, :, s0:s0 + width])
            for k in range(s0 // 512, (s0 + width) // 512):
                wsrc[(c, k)] = wraw[:, :, 512 * k - s0:512 * k - s0 + 512]

        def load_d(hh):
            nc.sync.dma_start(out=draw[hh][:].rearrange("q (n x) -> q n x", n=4), in_=dv[hh])

        def load_h(j):
            nc.sync.dma_start(out=hraw[j][:], in_=hv[j])

        def load_b():
            nc.sync.dma_start(out=brow[0:1, 0:1024], in_=dec_b.rearrange("(o n) p -> o (n p)", o=1))
            nc.sync.dma_start(out=brow[0:1, 1024:3072], in_=map_b.rearrange("(o s) -> o s", o=1))

        load_h(0)
        load_b()
        load_d(0)
        load_d(1)
        load_h(1)
        load_h(2)
        load_h(3)
        load_w(0, 0, 1024)
        load_w(0, 1024, 1024)
        load_w(1, 0, 2048)
        load_w(2, 0, 1024)
        load_w(2, 1024, 1024)
        load_w(3, 0, 1024)
        load_w(3, 1024, 1024)
        by = const.tile([P, 2048], BF16, name="by")

        decb = const.tile([P, 1024], BF16, name="decb")
        dgr = [const.tile([P, 2048], BF16, name="dgr%d" % hh, align_bytes=64) for hh in range(2)]
        dw = [const.tile([P, 512], U32, name="dw%d" % hh, align_bytes=64) for hh in range(2)]
        dsc = [const.tile([P, 512], U8, name="dsc%d" % hh, align_bytes=64) for hh in range(2)]
        hgr = [const.tile([P, 2048], BF16, name="hgr%d" % j, align_bytes=64) for j in range(4)]
        hw = [const.tile([P, 512], U32, name="hw%d" % j, align_bytes=64) for j in range(4)]
        hsc = [const.tile([P, 512], U8, name="hsc%d" % j, align_bytes=64) for j in range(4)]
        xrec = const.tile([P, 2048], BF16, name="xrec", align_bytes=64)
        xgr = const.tile([P, 2048], BF16, name="xgr", align_bytes=64)
        xw = const.tile([P, 512], U32, name="xw", align_bytes=64)
        xsc = const.tile([P, 512], U8, name="xsc", align_bytes=64)
        ov = out.rearrange("b c s -> (b c) s")
        live = {}

        def copy_on(eng, dst, src):
            if eng == "V":
                nc.vector.tensor_copy(out=dst, in_=src)
            else:
                nc.scalar.copy(out=dst, in_=src)

        def SPM(g):
            pb = psum.tile([P, 1024], BF16, name="pb", tag="ps")
            for e in range(2):
                nc.tensor.matmul(out=pb[:, 512 * e:512 * e + 512], lhsT=ones[:],
                                 rhs=brow[:, 1024 * g + 512 * e:1024 * g + 512 * e + 512],
                                 start=True, stop=True)
            live[("pb", g)] = pb

        def SPC(g):
            pb = live[("pb", g)]
            if g == 0:
                nc.scalar.copy(out=decb[:].rearrange("b (p n) -> b p n", n=8),
                               in_=pb[:].rearrange("b (n p) -> b p n", n=8))
            else:
                nc.scalar.copy(out=by[:, 1024 * g - 1024:1024 * g], in_=pb[:])

        def spread(g):
            SPM(g)
            SPC(g)

        def RD(hh):
            nc.vector.tensor_copy(
                out=dgr[hh][:].rearrange("q (n c i t) -> q n c t i", n=4, i=4, t=4),
                in_=draw[hh][:].rearrange("q (n t c i) -> q n c t i", n=4, t=4, i=4))

        def QD(hh):
            nc.vector.quantize_mx(out=dw[hh][:].bitcast(FP8X4), scales=dsc[hh][:], in_=dgr[hh][:])

        def TH1(j, l):
            words = hraw[j][:].bitcast(F32)
            tp = psum.tile([P, 2, 2, P], F32, name="tp", tag="ps")
            live[("tp", j, l)] = tp
            for w in range(2):
                base = 512 * w + 256 * l
                for u in range(2):
                    nc.tensor.transpose(tp[:, w, u, :], words[:, base + u:base + 256:2], ident[:])

        def TH(j):
            TH1(j, 0)
            TH1(j, 1)

        def EH1(eng, j, l):
            copy_on(eng, hgr[j][:, 1024 * l:1024 * l + 1024].bitcast(F32).rearrange("q (r v) -> q r v", v=4),
                    live[("tp", j, l)][:].rearrange("q w u r -> q r (w u)"))

        def EH(j):
            EH1("S", j, 0)
            EH1("S", j, 1)

        def QH(j):
            nc.vector.quantize_mx(out=hw[j][:].bitcast(FP8X4), scales=hsc[j][:], in_=hgr[j][:])

        def S1(j):
            for g in range(4):
                if j == 0:
                    live[("xb", g)] = accs.tile([P, 8, 64], F32, name="xb%d" % g, tag="acc%d" % g)
                l, pc = g // 2, g % 2
                for e in range(2):
                    n = 2 * j + e
                    a = 256 * l + 128 * e
                    b = 128 * (n % 4) + 64 * pc
                    nc.tensor.matmul_mx(
                        out=live[("xb", g)][:, n, :],
                        lhsT=hw[j][:, a:a + P].bitcast(FP8X4), lhsT_scale=hsc[j][:, a:a + P],
                        rhs=dw[n // 4][:, b:b + 64].bitcast(FP8X4), rhs_scale=dsc[n // 4][:, b:b + 64],
                        start=True, stop=True)

        def EX(g):
            nc.vector.tensor_tensor(
                out=xrec[:, 512 * g:512 * g + 512].rearrange("b (p n) -> b p n", n=8),
                in0=live[("xb", g)][:].rearrange("b n p -> b p n"),
                in1=decb[:, 512 * (g % 2):512 * (g % 2) + 512].rearrange("b (p n) -> b p n", n=8),
                op=ADD)

        def TX1(g):
            words = xrec[:].bitcast(F32)
            i, c = g // 2, g % 2
            if ("xt", i) not in live:
                live[("xt", i)] = psum.tile([P, 2, 2, P], F32, name="xt", tag="ps")
            base = 256 * g
            for u in range(2):
                nc.tensor.transpose(live[("xt", i)][:, c, u, :], words[:, base + u:base + 256:2], ident[:])

        def TX(i):
            TX1(2 * i)
            TX1(2 * i + 1)

        def EXT(i):
            nc.scalar.copy(
                out=xgr[:, 1024 * i:1024 * i + 1024].bitcast(F32).rearrange("q (c b u) -> q c b u", c=2, u=2),
                in_=live[("xt", i)][:].rearrange("q c u b -> q c b u"))

        def QX(i):
            nc.vector.quantize_mx(out=xw[:, 256 * i:256 * i + 256].bitcast(FP8X4),
                                  scales=xsc[:, 256 * i:256 * i + 256],
                                  in_=xgr[:, 1024 * i:1024 * i + 1024])

        def RW(eng, c, k, lo=0, hi=512):
            if (c, k // 2) not in live:
                live[(c, k // 2)] = stage.tile([P, 4096], BF16, name="wgr", align_bytes=64)
            base = 512 * (k % 2)
            dst = live[(c, k // 2)][:, 4 * (base + lo):4 * (base + hi)].rearrange("p (c i t) -> p c t i", i=4, t=4)
            src = wsrc[(c, k)][:, :, lo:hi].rearrange("p t (c i) -> p c t i", i=4)
            copy_on(eng, dst, src)

        def QP(c, g):
            ww = const.tile([P, 1024], U32, name="wwp%d_%d" % (c, g), align_bytes=64)
            wsc = const.tile([P, 1024], U8, name="wscp%d_%d" % (c, g), align_bytes=64)
            for e in range(2):
                live[("ww", c, 2 * g + e)] = (ww[:, 512 * e:512 * e + 512], wsc[:, 512 * e:512 * e + 512])
            nc.vector.quantize_mx(out=ww[:].bitcast(FP8X4), scales=wsc[:], in_=live[(c, g)][:])

        def QW(c, k):
            ww = const.tile([P, 512], U32, name="ww%d_%d" % (c, k), align_bytes=64)
            wsc = const.tile([P, 512], U8, name="wsc%d_%d" % (c, k), align_bytes=64)
            live[("ww", c, k)] = (ww[:], wsc[:])
            nc.vector.quantize_mx(out=ww[:].bitcast(FP8X4), scales=wsc[:],
                                  in_=live[(c, k // 2)][:, 2048 * (k % 2):2048 * (k % 2) + 2048])

        def MM(c, k):
            cnt = live.get(("n", k), 0)
            live[("n", k)] = cnt + 1
            if cnt == 0:
                live[("yacc", k)] = accs.tile([P, 512], F32, name="yacc%d" % k, tag="acc%d" % k)
            ww, wsc = live[("ww", c, k)]
            nc.tensor.matmul_mx(
                out=live[("yacc", k)][:],
                lhsT=xw[:, P * c:P * c + P].bitcast(FP8X4), lhsT_scale=xsc[:, P * c:P * c + P],
                rhs=ww.bitcast(FP8X4), rhs_scale=wsc,
                start=(cnt == 0), stop=(cnt == 3))

        def EY(k):
            yo = const.tile([P, 512], F32, name="yo%d" % k)
            nc.vector.tensor_tensor(out=yo[:], in0=live[("yacc", k)][:],
                                    in1=by[:, 512 * k:512 * k + 512], op=ADD)
            nc.sync.dma_start(out=ov[:, 512 * k:512 * k + 512], in_=yo[:])

        TH(0)
        EH(0)
        RD(0)
        spread(0)
        spread(1)
        spread(2)
        QH(0)
        QD(0)
        RD(1)
        S1(0)
        TH(1)
        QD(1)
        EH1("V", 1, 0)
        EH1("S", 1, 1)
        TH(2)
        EH1("S", 2, 0)
        EH1("S", 2, 1)
        QH(1)
        TH(3)
        EH1("V", 3, 0)
        EH1("S", 3, 1)
        S1(1)
        QH(2)
        QH(3)
        S1(2)
        S1(3)
        RW("S", 0, 0)
        RW("V", 0, 1)
        for g in range(4):
            EX(g)
            TX1(g)
        RW("S", 0, 2)
        QP(0, 0)
        EXT(0)
        EXT(1)
        RW("V", 0, 3)
        QX(0)
        QX(1)
        for k in range(2):
            MM(0, k)
        RW("S", 1, 0)
        QP(0, 1)
        for k in range(2, 4):
            MM(0, k)
        RW("V", 1, 1)
        pairs = [(c, g) for c in range(1, 4) for g in range(2)]
        for i in range(1, 5):
            c, g = pairs[i]
            RW("S", c, 2 * g)
            RW("V", c, 2 * g + 1)
            c, g = pairs[i - 1]
            QP(c, g)
            MM(c, 2 * g)
            MM(c, 2 * g + 1)
        RW("S", 3, 2)
        QW(3, 1)
        MM(3, 1)
        RW("V", 3, 3)
        QW(3, 0)
        MM(3, 0)
        QW(3, 3)
        MM(3, 3)
        EY(1)
        EY(0)
        QW(3, 2)
        MM(3, 2)
        EY(3)
        EY(2)
